import numpy as np
import ml_dtypes


def mxq(x, axis, fmt="e4m3"):
    dtype, down = {"e4m3": (ml_dtypes.float8_e4m3fn, 7), "e5m2": (ml_dtypes.float8_e5m2, 14)}[fmt]
    v = np.moveaxis(np.asarray(x, np.float32).astype(ml_dtypes.bfloat16).astype(np.float64), axis, -1)
    blocks = v.reshape(v.shape[:-1] + (-1, 32))
    amax = np.abs(blocks).max(-1, keepdims=True)
    byte = np.maximum(np.where(amax > 0, np.frexp(amax)[1] - 1 + 127, 0) - down, 1)
    scale = np.exp2(byte - 127.0)
    codes = (blocks / scale).astype(np.float32).astype(dtype).astype(np.float64)
    return np.moveaxis((codes * scale).reshape(v.shape), -1, axis)


WIDE = False


def mx_kscale(k):
    if not WIDE:
        return np.ones(k)
    levels = np.array([10, -10, 5, -5, 0])
    if k % 512:
        return np.exp2(np.random.permutation(np.resize(levels, k // 32))).repeat(32)
    a = np.empty((k // 512, 16))
    for p in range(k // 512):
        a[p, :8] = np.random.permutation(np.resize(levels, 8))
        for g in range(8):
            far = levels[np.abs(levels - a[p, g]) >= 10]
            a[p, g + 8] = far[np.random.randint(len(far))]
    return np.exp2(a.ravel()).repeat(32)


BF16 = ml_dtypes.bfloat16


def bf(x):
    return np.asarray(x, np.float32).astype(BF16)


def f64(x):
    return np.asarray(x).astype(np.float64)


B, D_IN, H = 256, 1024, 1024
QH = True


def sigmoid(v):
    return 1.0 / (1.0 + np.exp(-v))


def draw0():
    s = mx_kscale(D_IN)
    t = mx_kscale(H) if QH else np.ones(H)
    return {"x": bf(np.random.standard_normal((B, D_IN)) * s),
            "h_prev": bf(np.random.standard_normal((B, H)) * t),
            "c_prev": bf(np.random.standard_normal((B, H))),
            "W_all": bf(np.random.standard_normal((6, H, D_IN)) / np.sqrt(D_IN) / s),
            "b_all": bf(np.random.standard_normal((6, H)) * 0.3),
            "U_all": bf(np.random.standard_normal((6, H, H)) / np.sqrt(H) / t)}


def core(x, h_prev, c_prev, W_all, b_all, U_all):
    wx = (mxq(f64(x), 1, "e4m3") @ mxq(f64(W_all), 2, "e4m3").transpose(0, 2, 1)) + f64(b_all)[:, None, :]
    if QH:
        uh = mxq(f64(h_prev), 1, "e4m3") @ mxq(f64(U_all), 2, "e4m3").transpose(0, 2, 1)
    else:
        uh = f64(h_prev) @ f64(U_all).transpose(0, 2, 1)
    z = wx + uh
    i = sigmoid(z[0])
    f = sigmoid(z[1])
    o = sigmoid(z[2])
    g = np.tanh(z[3])
    m = wx[4] * uh[4]
    a = sigmoid(z[5])
    c_new = f * f64(c_prev) + i * g + a * m
    h_new = o * np.tanh(c_new)
    return (h_new, c_new)


def e4m3fn_bytes(y):
    return np.clip(np.asarray(y, np.float64), -448.0, 448.0).astype(np.float32).astype(ml_dtypes.float8_e4m3fn).view(np.uint8)


def e4m3fn_values(b):
    return np.asarray(b, np.uint8).view(ml_dtypes.float8_e4m3fn).astype(np.float64)


def setup_inputs():
    d = draw0()
    x0 = np.asarray(d['W_all']).astype(np.float64)
    s = (np.max(np.abs(x0), axis=(0, 1), keepdims=True) / 448.0).astype(np.float32)
    out = {}
    for k, v in d.items():
        if k == 'W_all':
            out['W_all_bytes'] = e4m3fn_bytes(x0 / s.astype(np.float64))
            out['W_all_scale'] = s
        else:
            out[k] = v
    return out


def reference(x, h_prev, c_prev, W_all_bytes, W_all_scale, b_all, U_all):
    return core(x, h_prev, c_prev, e4m3fn_values(W_all_bytes) * W_all_scale.astype(np.float64), b_all, U_all)

@@ -1,0 +1,360 @@
+from contextlib import ExitStack
+
+import concourse.mybir as mybir
+from concourse.masks import make_identity
+
+FLOPS = 2 * 256 * 1024 * 1024 * 12
+
+F32 = mybir.dt.float32
+BF16 = mybir.dt.bfloat16
+U32 = mybir.dt.uint32
+U8 = mybir.dt.uint8
+FP8 = mybir.dt.float8_e4m3fn
+FP8X4 = mybir.dt.float8_e4m3fn_x4
+ACT = mybir.ActivationFunctionType
+ALU = mybir.AluOpType
+
+P = 128
+B = 256
+K = 1024
+H = 1024
+NT = H // P
+NG = 3 * NT
+GATES = ((4, 5), (0, 3), (1, 2))
+AHEAD = 7
+
+
+def tile_xlstmcell_kernel(tc, x, h_prev, c_prev, W_all_bytes, W_all_scale, b_all, U_all, out_0, out_1):
+    nc = tc.nc
+    with ExitStack() as ctx:
+        const = ctx.enter_context(tc.tile_pool(name="const", bufs=1))
+        wpool = ctx.enter_context(tc.tile_pool(name="wpool", bufs=8))
+        upool = ctx.enter_context(tc.tile_pool(name="upool", bufs=8))
+        fpool = ctx.enter_context(tc.tile_pool(name="fpool", bufs=4))
+        gpool = ctx.enter_context(tc.tile_pool(name="gpool", bufs=4))
+        cpool = ctx.enter_context(tc.tile_pool(name="cpool", bufs=6))
+        epool = ctx.enter_context(tc.tile_pool(name="epool", bufs=2))
+        pst = ctx.enter_context(tc.psum_pool(name="pst", bufs=4))
+        psa = ctx.enter_context(tc.psum_pool(name="psa", bufs=4))
+        ctx.enter_context(tc.manual_schedule())
+
+        wb_t = {}
+        ub_t = {}
+        wf_t = {}
+        grp_t = {}
+        cod_t = {}
+        acc_t = {}
+        ep_t = {}
+
+        def gate_rows(dram, n):
+            j, pr = divmod(n, 3)
+            a, b = GATES[pr]
+            return dram[a : b + 1 : b - a, P * j : P * (j + 1), :].rearrange("q p k -> p q k")
+
+        def load_w(n):
+            wbytes = wpool.tile([P, 2, K], U8, name="wbytes")
+            nc.sync.dma_start(out=wbytes[:], in_=gate_rows(W_all_bytes, n))
+            wb_t[n] = wbytes
+
+        def load_u(n):
+            ubf = upool.tile([P, 2, K], BF16, name="ubf")
+            nc.sync.dma_start(out=ubf[:], in_=gate_rows(U_all, n))
+            ub_t[n] = ubf
+
+        def prep_turn(raw, ag):
+            for g in range(2):
+                tp = pst.tile([P, 512], F32, name="tp")
+                tpv = tp[:].rearrange("p (u b) -> p u b", u=2)
+                for bt in range(2):
+                    words = raw[:, bt, :].bitcast(F32)
+                    for u in range(2):
+                        nc.tensor.transpose(
+                            tpv[:, u, P * bt : P * (bt + 1)], words[:, 256 * g + u : 256 * (g + 1) : 2], ident[:]
+                        )
+                nc.scalar.copy(out=ag[:, g].bitcast(F32), in_=tp[:].rearrange("p (u b) -> p b u", u=2))
+
+        def prep_quant(ag, nm):
+            ac = const.tile([P, 2 * B], U32, name=nm + "c", align_bytes=64)
+            asc = const.tile([P, 2 * B], U8, name=nm + "s", align_bytes=64)
+            nc.vector.quantize_mx(
+                out=ac[:].bitcast(FP8X4), scales=asc[:], in_=ag[:].rearrange("p g b t -> p (g b t)")
+            )
+            return ac, asc
+
+        def product(n):
+            wfull = fpool.tile([P, 2, K], BF16, name="wfull")
+            if n < 2:
+                for i in range(2):
+                    nc.vector.tensor_tensor(
+                        out=wfull[:, i, :], in0=wb_t[n][:, i, :].bitcast(FP8), in1=sc2[:, 0, :], op=ALU.mult
+                    )
+            else:
+                nc.vector.tensor_tensor(
+                    out=wfull[:].rearrange("p q k -> p (q k)"),
+                    in0=wb_t[n][:].rearrange("p q k -> p (q k)").bitcast(FP8),
+                    in1=sc2[:].rearrange("p a k -> p (a k)"),
+                    op=ALU.mult,
+                )
+            wf_t[n] = wfull
+
+        def turn(n, units):
+            if n not in grp_t:
+                grp = gpool.tile([P, 4, 2, P, 4], BF16, name="grp", align_bytes=64)
+                grp_t[n] = grp
+            grp = grp_t[n]
+            for unit in units:
+                src = ub_t[n] if unit < 2 else wf_t[n]
+                words = src[:, unit % 2, :].bitcast(F32)
+                tp = pst.tile([P, 512], F32, name="tp")
+                tpv = tp[:].rearrange("p (g u r) -> p g u r", g=2, u=2)
+                for g in range(2):
+                    for u in range(2):
+                        nc.tensor.transpose(tpv[:, g, u, :], words[:, 256 * g + u : 256 * (g + 1) : 2], ident[:])
+                nc.scalar.copy(
+                    out=grp[:, unit].bitcast(F32), in_=tp[:].rearrange("p (g u r) -> p g r u", g=2, u=2)
+                )
+
+        def quantize(n):
+            codes = cpool.tile([P, 1024], U32, name="codes", align_bytes=64)
+            scl = cpool.tile([P, 1024], U8, name="scl", align_bytes=64)
+            nc.vector.quantize_mx(
+                out=codes[:].bitcast(FP8X4), scales=scl[:], in_=grp_t[n][:].rearrange("p a g r t -> p (a g r t)")
+            )
+            cod_t[n] = (codes, scl)
+
+        def mx_group(out, n, passes):
+            codes, scl = cod_t[n]
+            last = len(passes) - 1
+            for idx, (unit, g) in enumerate(passes):
+                ac, asc = acts[unit // 2]
+                off = (unit * 2 + g) * P
+                nc.tensor.matmul_mx(
+                    out=out,
+                    lhsT=codes[:, off : off + P].bitcast(FP8X4),
+                    lhsT_scale=scl[:, off : off + P],
+                    rhs=ac[:, g * B : (g + 1) * B].bitcast(FP8X4),
+                    rhs_scale=asc[:, g * B : (g + 1) * B],
+                    start=(idx == 0),
+                    stop=(idx == last),
+                )
+
+        def matmuls(n, part):
+            pr = n % 3
+            w_and_u = [(2 + part, 0), (2 + part, 1), (part, 0), (part, 1)]
+            if part == 0:
+                acc = psa.tile([P, 512], F32, name="acc")
+                acc_t[n] = [acc]
+                if pr == 0:
+                    mx_group(acc[:, 0:B], n, w_and_u[0:2])
+                    mx_group(acc[:, B : 2 * B], n, w_and_u[2:4])
+                else:
+                    mx_group(acc[:, 0:B], n, w_and_u)
+            elif pr == 0:
+                acc2 = psa.tile([P, 512], F32, name="acc")
+                acc_t[n].append(acc2)
+                mx_group(acc2[:, 0:B], n, w_and_u)
+            else:
+                mx_group(acc_t[n][0][:, B : 2 * B], n, w_and_u)
+
+        def gate_tanh(out, src, q, j):
+            col = q * NT + j
+            if q == 3:
+                nc.scalar.activation(out=out, in_=src, func=ACT.Tanh, bias=bfull[:, col : col + 1], scale=1.0)
+            else:
+                nc.scalar.activation(out=out, in_=src, func=ACT.Tanh, bias=bhalf[:, col : col + 1], scale=0.5)
+
+        def gates_scalar(n):
+            j, pr = divmod(n, 3)
+            e = ep_t.setdefault(j, {})
+            acc = acc_t[n][0]
+            if pr == 0:
+                t3 = epool.tile([P, 3, B], F32, name="t3")
+                e["t3"] = t3
+                u4 = epool.tile([P, B], F32, name="u4")
+                e["u4"] = u4
+                nc.scalar.copy(out=u4[:], in_=acc[:, B : 2 * B])
+                gate_tanh(t3[:, 2, :], acc_t[n][1][:, 0:B], 5, j)
+            elif pr == 1:
+                gate_tanh(e["t3"][:, 1, :], acc[:, 0:B], 0, j)
+                gate_tanh(y3[:, j, 1, :], acc[:, B : 2 * B], 3, j)
+            else:
+                gate_tanh(e["t3"][:, 0, :], acc[:, 0:B], 1, j)
+                to = epool.tile([P, B], F32, name="to")
+                e["to"] = to
+                gate_tanh(to[:], acc[:, B : 2 * B], 2, j)
+
+        def plus1_times(j, lo, hi):
+            e = ep_t[j]
+            nc.vector.scalar_tensor_tensor(
+                out=e["p3"][:, lo:hi, :].rearrange("p w b -> p (w b)"),
+                in0=e["t3"][:, lo:hi, :].rearrange("p w b -> p (w b)"),
+                scalar=1.0,
+                in1=y3[:, j, lo:hi, :].rearrange("p w b -> p (w b)"),
+                op0=ALU.add,
+                op1=ALU.mult,
+            )
+
+        def gates_vector(n):
+            j, pr = divmod(n, 3)
+            e = ep_t[j]
+            if pr == 0:
+                col = 4 * NT + j
+                nc.vector.scalar_tensor_tensor(
+                    out=y3[:, j, 2, :],
+                    in0=acc_t[n][0][:, 0:B],
+                    scalar=bfull[:, col : col + 1],
+                    in1=e["u4"][:],
+                    op0=ALU.add,
+                    op1=ALU.mult,
+                )
+                p3 = epool.tile([P, 3, B], F32, name="p3")
+                e["p3"] = p3
+            elif j == NT - 1:
+                if pr == 1:
+                    plus1_times(j, 1, 3)
+                else:
+                    plus1_times(j, 0, 1)
+            elif pr == 2:
+                plus1_times(j, 0, 3)
+
+        def finish_tensor(j):
+            e = ep_t[j]
+            tp = pst.tile([P, 512], F32, name="tp")
+            tpv = tp[:].rearrange("p (w t n) -> p w t n", w=2, t=2)
+            for bt in range(2):
+                for idx, w in enumerate((1, 2, 0)):
+                    nc.tensor.matmul(
+                        out=tpv[:, 0, bt, :],
+                        lhsT=e["p3"][:, w, P * bt : P * (bt + 1)],
+                        rhs=ident[:],
+                        is_transpose=True,
+                        start=(idx == 0),
+                        stop=(idx == 2),
+                    )
+            for bt in range(2):
+                nc.tensor.transpose(tpv[:, 1, bt, :], e["to"][:, P * bt : P * (bt + 1)], ident[:])
+            e["tpv"] = tpv
+
+        def finish_scalar(j):
+            e = ep_t[j]
+            tpv = e["tpv"]
+            tcn = epool.tile([P, 2, P], F32, name="tcn")
+            nc.scalar.activation(out=tcn[:], in_=tpv[:, 0], func=ACT.Tanh, scale=0.5)
+            ot = epool.tile([P, 2, P], F32, name="ot")
+            nc.scalar.activation(out=ot[:], in_=tpv[:, 1], func=ACT.Copy, bias=0.5, scale=0.5)
+            co = epool.tile([P, 2, P], F32, name="co")
+            nc.scalar.activation(out=co[:], in_=tpv[:, 0], func=ACT.Copy, scale=0.5)
+            cols = slice(P * j, P * (j + 1))
+            nc.sync.dma_start(out=out_1.rearrange("(t p) n -> p t n", p=P)[:, :, cols], in_=co[:])
+            e["tcn"] = tcn
+            e["ot"] = ot
+
+        def finish_vector(j):
+            e = ep_t[j]
+            ho = epool.tile([P, 2, P], F32, name="ho")
+            nc.vector.tensor_tensor(out=ho[:], in0=e["ot"][:], in1=e["tcn"][:], op=ALU.mult)
+            cols = slice(P * j, P * (j + 1))
+            nc.sync.dma_start(out=out_0.rearrange("(t p) n -> p t n", p=P)[:, :, cols], in_=ho[:])
+
+        warm = const.tile([P, 1], F32, name="warm")
+        warm2 = const.tile([P, 1], F32, name="warm2")
+        nc.vector.memset(warm[:], 0.0)
+        nc.scalar.activation(out=warm2[:], in_=warm[:], func=ACT.Tanh)
+        ident = const.tile([P, P], F32, name="ident")
+        make_identity(nc, ident[:])
+        identb = const.tile([P, P], BF16, name="identb")
+        make_identity(nc, identb[:])
+        brow = const.tile([P, P], BF16, name="brow")
+        nc.gpsimd.memset(brow[:], 0.0)
+
+        sc2 = const.tile([P, 2, K], F32, name="sc2")
+        scol = const.tile([P, 8], F32, name="scol")
+        nc.sync.dma_start(out=scol[:], in_=W_all_scale.rearrange("a b (p c) -> p (a b c)", c=8))
+        load_w(0)
+        load_u(0)
+        xraw = const.tile([P, 2, K], BF16, name="xraw")
+        nc.sync.dma_start(out=xraw[:], in_=x.rearrange("(t p) k -> p t k", p=P))
+        hraw = const.tile([P, 2, K], BF16, name="hraw")
+        nc.sync.dma_start(out=hraw[:], in_=h_prev.rearrange("(t p) k -> p t k", p=P))
+        load_w(1)
+        load_u(1)
+        craw = const.tile([P, 2, H], BF16, name="craw")
+        nc.sync.dma_start(out=craw[:], in_=c_prev.rearrange("(t p) n -> p t n", p=P))
+        nc.sync.dma_start(out=brow[0 : 6 * NT, :], in_=b_all.rearrange("q (j p) -> (q j) p", p=P))
+        for n in range(2, AHEAD - 3):
+            load_w(n)
+            load_u(n)
+
+        xg = const.tile([P, 2, B, 4], BF16, name="xg", align_bytes=64)
+        hg = const.tile([P, 2, B, 4], BF16, name="hg", align_bytes=64)
+        y3 = const.tile([P, NT, 3, B], F32, name="y3")
+        bfull = const.tile([P, 6 * NT], F32, name="bfull")
+        bhalf = const.tile([P, 6 * NT], F32, name="bhalf")
+
+        def head_small():
+            for half in range(2):
+                tpb = pst.tile([P, 1024], BF16, name="tp")
+                tpbv = tpb[:].rearrange("p (j b) -> p j b", j=4)
+                for jj in range(4):
+                    for bt in range(2):
+                        nc.tensor.transpose(
+                            tpbv[:, jj, P * bt : P * (bt + 1)],
+                            craw[:, bt, P * (4 * half + jj) : P * (4 * half + jj + 1)],
+                            identb[:],
+                        )
+                nc.scalar.copy(out=y3[:, 4 * half : 4 * half + 4, 0, :], in_=tpbv)
+            tpb = pst.tile([P, 1024], BF16, name="tp")
+            nc.tensor.transpose(tpb[:, 0:P], brow[:], identb[:])
+            nc.scalar.copy(out=bfull[:], in_=tpb[:, 0 : 6 * NT])
+            nc.scalar.activation(out=bhalf[:], in_=tpb[:, 0 : 6 * NT], func=ACT.Copy, scale=0.5)
+
+        acts = []
+
+        for hb in range(2):
+            tp = pst.tile([P, 512], F32, name="tp")
+            tpv = tp[:].rearrange("p (c n) -> p c n", c=4)
+            for c in range(4):
+                nc.tensor.transpose(tpv[:, c, :], scol[:, 4 * hb + c : 4 * hb + c + 1].to_broadcast([P, P]), ident[:])
+            dst = sc2[:, 0, :].rearrange("p (n c) -> p n c", c=8)[:, :, 4 * hb : 4 * hb + 4]
+            if hb == 0:
+                nc.vector.tensor_copy(out=dst, in_=tp[:].rearrange("p (c n) -> p n c", c=4))
+            else:
+                nc.scalar.copy(out=dst, in_=tp[:].rearrange("p (c n) -> p n c", c=4))
+
+        for n in range(-3, NG + 3):
+            if AHEAD - 3 <= n + AHEAD < NG:
+                load_w(n + AHEAD)
+                load_u(n + AHEAD)
+            if n >= 5 and (n - 5) % 3 == 0:
+                finish_scalar((n - 5) // 3)
+            if 0 <= n - 1 < NG:
+                gates_scalar(n - 1)
+            if 0 <= n + 3 < NG:
+                product(n + 3)
+            if n == -3:
+                turn(0, (0, 1))
+                prep_turn(xraw, xg)
+                prep_turn(hraw, hg)
+            if n == -2:
+                turn(0, (2, 3))
+                nc.scalar.copy(out=sc2[:, 1, :], in_=sc2[:, 0, :])
+                acts.append(prep_quant(hg, "ha"))
+                acts.append(prep_quant(xg, "xa"))
+            if 1 <= n + 2 < NG:
+                turn(n + 2, (0, 1))
+            if 0 <= n < NG:
+                matmuls(n, 0)
+            if 1 <= n + 2 < NG:
+                turn(n + 2, (2, 3))
+            if n == -1:
+                head_small()
+            if n >= 4 and (n - 4) % 3 == 0 and (n - 4) // 3 < NT:
+                finish_tensor((n - 4) // 3)
+            if 0 <= n + 1 < NG:
+                quantize(n + 1)
+            if 0 <= n < NG:
+                matmuls(n, 1)
+            if 0 <= n - 1 < NG:
+                gates_vector(n - 1)
+            if n >= 5 and (n - 5) % 3 == 0:
+                finish_vector((n - 5) // 3)

@@ -35,7 +35,8 @@ def tile_xlstmcell_kernel(tc, x, h_prev, c_prev, W_all_bytes, W_all_scale, b_all
         cpool = ctx.enter_context(tc.tile_pool(name="cpool", bufs=6))
         epool = ctx.enter_context(tc.tile_pool(name="epool", bufs=2))
         pst = ctx.enter_context(tc.psum_pool(name="pst", bufs=4))
-        psa = ctx.enter_context(tc.psum_pool(name="psa", bufs=4))
+        psa = ctx.enter_context(tc.psum_pool(name="psa", bufs=3))
+        psf = ctx.enter_context(tc.psum_pool(name="psf", bufs=1))
         ctx.enter_context(tc.manual_schedule())
 
         wb_t = {}
@@ -83,7 +84,14 @@ def tile_xlstmcell_kernel(tc, x, h_prev, c_prev, W_all_bytes, W_all_scale, b_all
 
         def product(n):
             wfull = fpool.tile([P, 2, K], BF16, name="wfull")
-            if n < 2:
+            if n == 0:
+                for hb in range(2):
+                    cols = slice(512 * hb, 512 * (hb + 1))
+                    for i in range(2):
+                        nc.vector.tensor_tensor(
+                            out=wfull[:, i, cols], in0=wb_t[n][:, i, cols].bitcast(FP8), in1=sc2[:, 0, cols], op=ALU.mult
+                        )
+            elif n == 1:
                 for i in range(2):
                     nc.vector.tensor_tensor(
                         out=wfull[:, i, :], in0=wb_t[n][:, i, :].bitcast(FP8), in1=sc2[:, 0, :], op=ALU.mult
@@ -156,42 +164,38 @@ def tile_xlstmcell_kernel(tc, x, h_prev, c_prev, W_all_bytes, W_all_scale, b_all
             else:
                 mx_group(acc_t[n][0][:, B : 2 * B], n, w_and_u)
 
-        def gate_tanh(out, src, q, j):
+        def gate_act(out, src, q, j):
             col = q * NT + j
-            if q == 3:
-                nc.scalar.activation(out=out, in_=src, func=ACT.Tanh, bias=bfull[:, col : col + 1], scale=1.0)
-            else:
-                nc.scalar.activation(out=out, in_=src, func=ACT.Tanh, bias=bhalf[:, col : col + 1], scale=0.5)
+            func = ACT.Tanh if q == 3 else ACT.Sigmoid
+            nc.scalar.activation(out=out, in_=src, func=func, bias=bfull[:, col : col + 1], scale=1.0)
 
         def gates_scalar(n):
             j, pr = divmod(n, 3)
             e = ep_t.setdefault(j, {})
             acc = acc_t[n][0]
             if pr == 0:
-                t3 = epool.tile([P, 3, B], F32, name="t3")
-                e["t3"] = t3
+                s3 = epool.tile([P, 3, B], F32, name="s3")
+                e["s3"] = s3
                 u4 = epool.tile([P, B], F32, name="u4")
                 e["u4"] = u4
                 nc.scalar.copy(out=u4[:], in_=acc[:, B : 2 * B])
-                gate_tanh(t3[:, 2, :], acc_t[n][1][:, 0:B], 5, j)
+                gate_act(s3[:, 2, :], acc_t[n][1][:, 0:B], 5, j)
             elif pr == 1:
-                gate_tanh(e["t3"][:, 1, :], acc[:, 0:B], 0, j)
-                gate_tanh(y3[:, j, 1, :], acc[:, B : 2 * B], 3, j)
+                gate_act(e["s3"][:, 1, :], acc[:, 0:B], 0, j)
+                gate_act(y3[:, j, 1, :], acc[:, B : 2 * B], 3, j)
             else:
-                gate_tanh(e["t3"][:, 0, :], acc[:, 0:B], 1, j)
-                to = epool.tile([P, B], F32, name="to")
-                e["to"] = to
-                gate_tanh(to[:], acc[:, B : 2 * B], 2, j)
+                gate_act(e["s3"][:, 0, :], acc[:, 0:B], 1, j)
+                so = epool.tile([P, B], F32, name="so")
+                e["so"] = so
+                gate_act(so[:], acc[:, B : 2 * B], 2, j)
 
-        def plus1_times(j, lo, hi):
+        def gate_times(j, lo, hi):
             e = ep_t[j]
-            nc.vector.scalar_tensor_tensor(
+            nc.vector.tensor_tensor(
                 out=e["p3"][:, lo:hi, :].rearrange("p w b -> p (w b)"),
-                in0=e["t3"][:, lo:hi, :].rearrange("p w b -> p (w b)"),
-                scalar=1.0,
+                in0=e["s3"][:, lo:hi, :].rearrange("p w b -> p (w b)"),
                 in1=y3[:, j, lo:hi, :].rearrange("p w b -> p (w b)"),
-                op0=ALU.add,
-                op1=ALU.mult,
+                op=ALU.mult,
             )
 
         def gates_vector(n):
@@ -211,15 +215,18 @@ def tile_xlstmcell_kernel(tc, x, h_prev, c_prev, W_all_bytes, W_all_scale, b_all
                 e["p3"] = p3
             elif j == NT - 1:
                 if pr == 1:
-                    plus1_times(j, 1, 3)
+                    gate_times(j, 1, 3)
                 else:
-                    plus1_times(j, 0, 1)
+                    gate_times(j, 0, 1)
             elif pr == 2:
-                plus1_times(j, 0, 3)
+                gate_times(j, 0, 3)
 
         def finish_tensor(j):
             e = ep_t[j]
-            tp = pst.tile([P, 512], F32, name="tp")
+            if j == NT - 1:
+                tp = pst.tile([P, 512], F32, name="tp")
+            else:
+                tp = psf.tile([P, 512], F32, name="fin")
             tpv = tp[:].rearrange("p (w t n) -> p w t n", w=2, t=2)
             for bt in range(2):
                 for idx, w in enumerate((1, 2, 0)):
@@ -232,34 +239,31 @@ def tile_xlstmcell_kernel(tc, x, h_prev, c_prev, W_all_bytes, W_all_scale, b_all
                         stop=(idx == 2),
                     )
             for bt in range(2):
-                nc.tensor.transpose(tpv[:, 1, bt, :], e["to"][:, P * bt : P * (bt + 1)], ident[:])
+                nc.tensor.transpose(tpv[:, 1, bt, :], e["so"][:, P * bt : P * (bt + 1)], ident[:])
             e["tpv"] = tpv
 
         def finish_scalar(j):
             e = ep_t[j]
             tpv = e["tpv"]
             tcn = epool.tile([P, 2, P], F32, name="tcn")
-            nc.scalar.activation(out=tcn[:], in_=tpv[:, 0], func=ACT.Tanh, scale=0.5)
-            ot = epool.tile([P, 2, P], F32, name="ot")
-            nc.scalar.activation(out=ot[:], in_=tpv[:, 1], func=ACT.Copy, bias=0.5, scale=0.5)
+            nc.scalar.activation(out=tcn[:], in_=tpv[:, 0], func=ACT.Tanh)
             co = epool.tile([P, 2, P], F32, name="co")
-            nc.scalar.activation(out=co[:], in_=tpv[:, 0], func=ACT.Copy, scale=0.5)
+            nc.scalar.copy(out=co[:], in_=tpv[:, 0])
             cols = slice(P * j, P * (j + 1))
             nc.sync.dma_start(out=out_1.rearrange("(t p) n -> p t n", p=P)[:, :, cols], in_=co[:])
             e["tcn"] = tcn
-            e["ot"] = ot
 
         def finish_vector(j):
             e = ep_t[j]
             ho = epool.tile([P, 2, P], F32, name="ho")
-            nc.vector.tensor_tensor(out=ho[:], in0=e["ot"][:], in1=e["tcn"][:], op=ALU.mult)
+            nc.vector.tensor_tensor(out=ho[:], in0=e["tpv"][:, 1], in1=e["tcn"][:], op=ALU.mult)
             cols = slice(P * j, P * (j + 1))
             nc.sync.dma_start(out=out_0.rearrange("(t p) n -> p t n", p=P)[:, :, cols], in_=ho[:])
 
         warm = const.tile([P, 1], F32, name="warm")
         warm2 = const.tile([P, 1], F32, name="warm2")
         nc.vector.memset(warm[:], 0.0)
-        nc.scalar.activation(out=warm2[:], in_=warm[:], func=ACT.Tanh)
+        nc.scalar.activation(out=warm2[:], in_=warm[:], func=ACT.Sigmoid)
         ident = const.tile([P, P], F32, name="ident")
         make_identity(nc, ident[:])
         identb = const.tile([P, P], BF16, name="identb")
@@ -268,8 +272,8 @@ def tile_xlstmcell_kernel(tc, x, h_prev, c_prev, W_all_bytes, W_all_scale, b_all
         nc.gpsimd.memset(brow[:], 0.0)
 
         sc2 = const.tile([P, 2, K], F32, name="sc2")
-        scol = const.tile([P, 8], F32, name="scol")
-        nc.sync.dma_start(out=scol[:], in_=W_all_scale.rearrange("a b (p c) -> p (a b c)", c=8))
+        scol = const.tile([P, 2, 4], F32, name="scol")
+        nc.sync.dma_start(out=scol[:], in_=W_all_scale.rearrange("a b (h p c) -> p (a b h) c", p=P, c=4))
         load_w(0)
         load_u(0)
         xraw = const.tile([P, 2, K], BF16, name="xraw")
@@ -289,7 +293,6 @@ def tile_xlstmcell_kernel(tc, x, h_prev, c_prev, W_all_bytes, W_all_scale, b_all
         hg = const.tile([P, 2, B, 4], BF16, name="hg", align_bytes=64)
         y3 = const.tile([P, NT, 3, B], F32, name="y3")
         bfull = const.tile([P, 6 * NT], F32, name="bfull")
-        bhalf = const.tile([P, 6 * NT], F32, name="bhalf")
 
         def head_small():
             for half in range(2):
@@ -306,7 +309,6 @@ def tile_xlstmcell_kernel(tc, x, h_prev, c_prev, W_all_bytes, W_all_scale, b_all
             tpb = pst.tile([P, 1024], BF16, name="tp")
             nc.tensor.transpose(tpb[:, 0:P], brow[:], identb[:])
             nc.scalar.copy(out=bfull[:], in_=tpb[:, 0 : 6 * NT])
-            nc.scalar.activation(out=bhalf[:], in_=tpb[:, 0 : 6 * NT], func=ACT.Copy, scale=0.5)
 
         acts = []
 
@@ -314,14 +316,14 @@ def tile_xlstmcell_kernel(tc, x, h_prev, c_prev, W_all_bytes, W_all_scale, b_all
             tp = pst.tile([P, 512], F32, name="tp")
             tpv = tp[:].rearrange("p (c n) -> p c n", c=4)
             for c in range(4):
-                nc.tensor.transpose(tpv[:, c, :], scol[:, 4 * hb + c : 4 * hb + c + 1].to_broadcast([P, P]), ident[:])
-            dst = sc2[:, 0, :].rearrange("p (n c) -> p n c", c=8)[:, :, 4 * hb : 4 * hb + 4]
+                nc.tensor.transpose(tpv[:, c, :], scol[:, hb, c : c + 1].to_broadcast([P, P]), ident[:])
+            dst = sc2[:, 0, 512 * hb : 512 * (hb + 1)].rearrange("p (n c) -> p n c", c=4)
             if hb == 0:
                 nc.vector.tensor_copy(out=dst, in_=tp[:].rearrange("p (c n) -> p n c", c=4))
             else:
                 nc.scalar.copy(out=dst, in_=tp[:].rearrange("p (c n) -> p n c", c=4))
 
-        for n in range(-3, NG + 3):
+        for n in range(-3, NG - 4):
             if AHEAD - 3 <= n + AHEAD < NG:
                 load_w(n + AHEAD)
                 load_u(n + AHEAD)
@@ -358,3 +360,40 @@ def tile_xlstmcell_kernel(tc, x, h_prev, c_prev, W_all_bytes, W_all_scale, b_all
                 gates_vector(n - 1)
             if n >= 5 and (n - 5) % 3 == 0:
                 finish_vector((n - 5) // 3)
+
+        finish_scalar(NT - 3)
+        gates_scalar(NG - 5)
+        product(NG - 1)
+        turn(NG - 2, (0, 1))
+        matmuls(NG - 4, 0)
+        turn(NG - 2, (2, 3))
+        quantize(NG - 3)
+        matmuls(NG - 4, 1)
+
+        gates_scalar(NG - 4)
+        turn(NG - 1, (0, 1))
+        turn(NG - 1, (2, 3))
+        quantize(NG - 2)
+        matmuls(NG - 3, 0)
+        matmuls(NG - 3, 1)
+
+        gates_scalar(NG - 3)
+        gates_vector(NG - 3)
+        quantize(NG - 1)
+        matmuls(NG - 2, 0)
+        matmuls(NG - 2, 1)
+        finish_vector(NT - 3)
+        gates_vector(NG - 4)
+
+        gates_scalar(NG - 2)
+        matmuls(NG - 1, 0)
+        matmuls(NG - 1, 1)
+        finish_tensor(NT - 2)
+        gates_vector(NG - 2)
+        gates_scalar(NG - 1)
+        gates_vector(NG - 1)
+        finish_scalar(NT - 2)
+        finish_tensor(NT - 1)
+        finish_vector(NT - 2)
+        finish_scalar(NT - 1)
+        finish_vector(NT - 1)

@@ -22,6 +22,8 @@ NT = H // P
 NG = 3 * NT
 GATES = ((4, 5), (0, 3), (1, 2))
 AHEAD = 7
+EARLY = 4
+POS = (0, 2, 1, 3)
 
 
 def tile_xlstmcell_kernel(tc, x, h_prev, c_prev, W_all_bytes, W_all_scale, b_all, U_all, out_0, out_1):
@@ -31,11 +33,12 @@ def tile_xlstmcell_kernel(tc, x, h_prev, c_prev, W_all_bytes, W_all_scale, b_all
         wpool = ctx.enter_context(tc.tile_pool(name="wpool", bufs=8))
         upool = ctx.enter_context(tc.tile_pool(name="upool", bufs=8))
         fpool = ctx.enter_context(tc.tile_pool(name="fpool", bufs=4))
-        gpool = ctx.enter_context(tc.tile_pool(name="gpool", bufs=4))
+        gpool = ctx.enter_context(tc.tile_pool(name="gpool", bufs=6))
         cpool = ctx.enter_context(tc.tile_pool(name="cpool", bufs=6))
         epool = ctx.enter_context(tc.tile_pool(name="epool", bufs=2))
-        pst = ctx.enter_context(tc.psum_pool(name="pst", bufs=4))
-        psa = ctx.enter_context(tc.psum_pool(name="psa", bufs=3))
+        opool = ctx.enter_context(tc.tile_pool(name="opool", bufs=3))
+        pst = ctx.enter_context(tc.psum_pool(name="pst", bufs=3))
+        psa = ctx.enter_context(tc.psum_pool(name="psa", bufs=4))
         psf = ctx.enter_context(tc.psum_pool(name="psf", bufs=1))
         ctx.enter_context(tc.manual_schedule())
 
@@ -43,6 +46,7 @@ def tile_xlstmcell_kernel(tc, x, h_prev, c_prev, W_all_bytes, W_all_scale, b_all
         ub_t = {}
         wf_t = {}
         grp_t = {}
+        turned = set()
         cod_t = {}
         acc_t = {}
         ep_t = {}
@@ -91,7 +95,7 @@ def tile_xlstmcell_kernel(tc, x, h_prev, c_prev, W_all_bytes, W_all_scale, b_all
                         nc.vector.tensor_tensor(
                             out=wfull[:, i, cols], in0=wb_t[n][:, i, cols].bitcast(FP8), in1=sc2[:, 0, cols], op=ALU.mult
                         )
-            elif n == 1:
+            elif n < 5 or n == NG - 1:
                 for i in range(2):
                     nc.vector.tensor_tensor(
                         out=wfull[:, i, :], in0=wb_t[n][:, i, :].bitcast(FP8), in1=sc2[:, 0, :], op=ALU.mult
@@ -111,6 +115,9 @@ def tile_xlstmcell_kernel(tc, x, h_prev, c_prev, W_all_bytes, W_all_scale, b_all
                 grp_t[n] = grp
             grp = grp_t[n]
             for unit in units:
+                if (n, unit) in turned:
+                    continue
+                turned.add((n, unit))
                 src = ub_t[n] if unit < 2 else wf_t[n]
                 words = src[:, unit % 2, :].bitcast(F32)
                 tp = pst.tile([P, 512], F32, name="tp")
@@ -119,15 +126,24 @@ def tile_xlstmcell_kernel(tc, x, h_prev, c_prev, W_all_bytes, W_all_scale, b_all
                     for u in range(2):
                         nc.tensor.transpose(tpv[:, g, u, :], words[:, 256 * g + u : 256 * (g + 1) : 2], ident[:])
                 nc.scalar.copy(
-                    out=grp[:, unit].bitcast(F32), in_=tp[:].rearrange("p (g u r) -> p g r u", g=2, u=2)
+                    out=grp[:, POS[unit]].bitcast(F32), in_=tp[:].rearrange("p (g u r) -> p g r u", g=2, u=2)
                 )
 
         def quantize(n):
             codes = cpool.tile([P, 1024], U32, name="codes", align_bytes=64)
             scl = cpool.tile([P, 1024], U8, name="scl", align_bytes=64)
-            nc.vector.quantize_mx(
-                out=codes[:].bitcast(FP8X4), scales=scl[:], in_=grp_t[n][:].rearrange("p a g r t -> p (a g r t)")
-            )
+            if n == NG - 1:
+                for i in range(2):
+                    cols = slice(512 * i, 512 * (i + 1))
+                    nc.vector.quantize_mx(
+                        out=codes[:, cols].bitcast(FP8X4),
+                        scales=scl[:, cols],
+                        in_=grp_t[n][:, 2 * i : 2 * i + 2].rearrange("p a g r t -> p (a g r t)"),
+                    )
+            else:
+                nc.vector.quantize_mx(
+                    out=codes[:].bitcast(FP8X4), scales=scl[:], in_=grp_t[n][:].rearrange("p a g r t -> p (a g r t)")
+                )
             cod_t[n] = (codes, scl)
 
         def mx_group(out, n, passes):
@@ -135,7 +151,7 @@ def tile_xlstmcell_kernel(tc, x, h_prev, c_prev, W_all_bytes, W_all_scale, b_all
             last = len(passes) - 1
             for idx, (unit, g) in enumerate(passes):
                 ac, asc = acts[unit // 2]
-                off = (unit * 2 + g) * P
+                off = (POS[unit] * 2 + g) * P
                 nc.tensor.matmul_mx(
                     out=out,
                     lhsT=codes[:, off : off + P].bitcast(FP8X4),
@@ -150,7 +166,10 @@ def tile_xlstmcell_kernel(tc, x, h_prev, c_prev, W_all_bytes, W_all_scale, b_all
             pr = n % 3
             w_and_u = [(2 + part, 0), (2 + part, 1), (part, 0), (part, 1)]
             if part == 0:
-                acc = psa.tile([P, 512], F32, name="acc")
+                if n == NG - 1:
+                    acc = pst.tile([P, 512], F32, name="tp")
+                else:
+                    acc = psa.tile([P, 512], F32, name="acc")
                 acc_t[n] = [acc]
                 if pr == 0:
                     mx_group(acc[:, 0:B], n, w_and_u[0:2])
@@ -223,40 +242,43 @@ def tile_xlstmcell_kernel(tc, x, h_prev, c_prev, W_all_bytes, W_all_scale, b_all
 
         def finish_tensor(j):
             e = ep_t[j]
-            if j == NT - 1:
+            if j >= NT - 2:
                 tp = pst.tile([P, 512], F32, name="tp")
             else:
                 tp = psf.tile([P, 512], F32, name="fin")
             tpv = tp[:].rearrange("p (w t n) -> p w t n", w=2, t=2)
+            e["ct"] = tpv[:, 0]
+            e["ot"] = tpv[:, 1]
+            if j == NT - 1:
+                tpo = pst.tile([P, 512], F32, name="tp")
+                e["ot"] = tpo[:].rearrange("p (w t n) -> p w t n", w=2, t=2)[:, 0]
+            for bt in range(2):
+                nc.tensor.transpose(e["ot"][:, bt, :], e["so"][:, P * bt : P * (bt + 1)], ident[:])
             for bt in range(2):
                 for idx, w in enumerate((1, 2, 0)):
                     nc.tensor.matmul(
-                        out=tpv[:, 0, bt, :],
+                        out=e["ct"][:, bt, :],
                         lhsT=e["p3"][:, w, P * bt : P * (bt + 1)],
                         rhs=ident[:],
                         is_transpose=True,
                         start=(idx == 0),
                         stop=(idx == 2),
                     )
-            for bt in range(2):
-                nc.tensor.transpose(tpv[:, 1, bt, :], e["so"][:, P * bt : P * (bt + 1)], ident[:])
-            e["tpv"] = tpv
 
         def finish_scalar(j):
             e = ep_t[j]
-            tpv = e["tpv"]
             tcn = epool.tile([P, 2, P], F32, name="tcn")
-            nc.scalar.activation(out=tcn[:], in_=tpv[:, 0], func=ACT.Tanh)
-            co = epool.tile([P, 2, P], F32, name="co")
-            nc.scalar.copy(out=co[:], in_=tpv[:, 0])
+            nc.scalar.activation(out=tcn[:], in_=e["ct"], func=ACT.Tanh)
+            co = opool.tile([P, 2, P], F32, name="co")
+            nc.scalar.copy(out=co[:], in_=e["ct"])
             cols = slice(P * j, P * (j + 1))
             nc.sync.dma_start(out=out_1.rearrange("(t p) n -> p t n", p=P)[:, :, cols], in_=co[:])
             e["tcn"] = tcn
 
         def finish_vector(j):
             e = ep_t[j]
-            ho = epool.tile([P, 2, P], F32, name="ho")
-            nc.vector.tensor_tensor(out=ho[:], in0=e["tpv"][:, 1], in1=e["tcn"][:], op=ALU.mult)
+            ho = opool.tile([P, 2, P], F32, name="ho")
+            nc.vector.tensor_tensor(out=ho[:], in0=e["ot"], in1=e["tcn"][:], op=ALU.mult)
             cols = slice(P * j, P * (j + 1))
             nc.sync.dma_start(out=out_0.rearrange("(t p) n -> p t n", p=P)[:, :, cols], in_=ho[:])
 
@@ -294,7 +316,7 @@ def tile_xlstmcell_kernel(tc, x, h_prev, c_prev, W_all_bytes, W_all_scale, b_all
         y3 = const.tile([P, NT, 3, B], F32, name="y3")
         bfull = const.tile([P, 6 * NT], F32, name="bfull")
 
-        def head_small():
+        def turn_c():
             for half in range(2):
                 tpb = pst.tile([P, 1024], BF16, name="tp")
                 tpbv = tpb[:].rearrange("p (j b) -> p j b", j=4)
@@ -306,6 +328,8 @@ def tile_xlstmcell_kernel(tc, x, h_prev, c_prev, W_all_bytes, W_all_scale, b_all
                             identb[:],
                         )
                 nc.scalar.copy(out=y3[:, 4 * half : 4 * half + 4, 0, :], in_=tpbv)
+
+        def turn_b():
             tpb = pst.tile([P, 1024], BF16, name="tp")
             nc.tensor.transpose(tpb[:, 0:P], brow[:], identb[:])
             nc.scalar.copy(out=bfull[:], in_=tpb[:, 0 : 6 * NT])
@@ -323,6 +347,9 @@ def tile_xlstmcell_kernel(tc, x, h_prev, c_prev, W_all_bytes, W_all_scale, b_all
             else:
                 nc.scalar.copy(out=dst, in_=tp[:].rearrange("p (c n) -> p n c", c=4))
 
+        u_units = [(m, i) for m in range(1, NG) for i in range(2)]
+        u_done = 0
+        extra = 0
         for n in range(-3, NG - 4):
             if AHEAD - 3 <= n + AHEAD < NG:
                 load_w(n + AHEAD)
@@ -339,17 +366,23 @@ def tile_xlstmcell_kernel(tc, x, h_prev, c_prev, W_all_bytes, W_all_scale, b_all
                 prep_turn(hraw, hg)
             if n == -2:
                 turn(0, (2, 3))
-                nc.scalar.copy(out=sc2[:, 1, :], in_=sc2[:, 0, :])
-                acts.append(prep_quant(hg, "ha"))
                 acts.append(prep_quant(xg, "xa"))
-            if 1 <= n + 2 < NG:
-                turn(n + 2, (0, 1))
+                acts.insert(0, prep_quant(hg, "ha"))
+            if n >= 2 and (n - 4) % 3 != 0 and extra < EARLY:
+                extra += 1
+            while u_done < min(2 * (n + 2) + extra, len(u_units)):
+                turn(u_units[u_done][0], u_units[u_done][1:2])
+                u_done += 1
             if 0 <= n < NG:
                 matmuls(n, 0)
             if 1 <= n + 2 < NG:
                 turn(n + 2, (2, 3))
             if n == -1:
-                head_small()
+                turn_b()
+            if n == 1:
+                nc.scalar.copy(out=sc2[:, 1, :], in_=sc2[:, 0, :])
+            if n == 2:
+                turn_c()
             if n >= 4 and (n - 4) % 3 == 0 and (n - 4) // 3 < NT:
                 finish_tensor((n - 4) // 3)
             if 0 <= n + 1 < NG:
@@ -369,29 +402,26 @@ def tile_xlstmcell_kernel(tc, x, h_prev, c_prev, W_all_bytes, W_all_scale, b_all
         turn(NG - 2, (2, 3))
         quantize(NG - 3)
         matmuls(NG - 4, 1)
-
         gates_scalar(NG - 4)
-        turn(NG - 1, (0, 1))
-        turn(NG - 1, (2, 3))
+        turn(NG - 1, (0, 2))
+        turn(NG - 1, (1, 3))
         quantize(NG - 2)
         matmuls(NG - 3, 0)
         matmuls(NG - 3, 1)
-
-        gates_scalar(NG - 3)
-        gates_vector(NG - 3)
         quantize(NG - 1)
+        gates_scalar(NG - 3)
         matmuls(NG - 2, 0)
         matmuls(NG - 2, 1)
-        finish_vector(NT - 3)
+        gates_vector(NG - 3)
         gates_vector(NG - 4)
-
         gates_scalar(NG - 2)
         matmuls(NG - 1, 0)
         matmuls(NG - 1, 1)
-        finish_tensor(NT - 2)
         gates_vector(NG - 2)
         gates_scalar(NG - 1)
         gates_vector(NG - 1)
+        finish_tensor(NT - 2)
+        finish_vector(NT - 3)
         finish_scalar(NT - 2)
         finish_tensor(NT - 1)
         finish_vector(NT - 2)

@@ -37,8 +37,8 @@ def tile_xlstmcell_kernel(tc, x, h_prev, c_prev, W_all_bytes, W_all_scale, b_all
         cpool = ctx.enter_context(tc.tile_pool(name="cpool", bufs=6))
         epool = ctx.enter_context(tc.tile_pool(name="epool", bufs=2))
         opool = ctx.enter_context(tc.tile_pool(name="opool", bufs=3))
-        pst = ctx.enter_context(tc.psum_pool(name="pst", bufs=3))
-        psa = ctx.enter_context(tc.psum_pool(name="psa", bufs=4))
+        pst = ctx.enter_context(tc.psum_pool(name="pst", bufs=4))
+        psa = ctx.enter_context(tc.psum_pool(name="psa", bufs=3))
         psf = ctx.enter_context(tc.psum_pool(name="psf", bufs=1))
         ctx.enter_context(tc.manual_schedule())
 

@@ -37,9 +37,8 @@ def tile_xlstmcell_kernel(tc, x, h_prev, c_prev, W_all_bytes, W_all_scale, b_all
         cpool = ctx.enter_context(tc.tile_pool(name="cpool", bufs=6))
         epool = ctx.enter_context(tc.tile_pool(name="epool", bufs=2))
         opool = ctx.enter_context(tc.tile_pool(name="opool", bufs=3))
-        pst = ctx.enter_context(tc.psum_pool(name="pst", bufs=4))
+        pst = ctx.enter_context(tc.psum_pool(name="pst", bufs=5))
         psa = ctx.enter_context(tc.psum_pool(name="psa", bufs=3))
-        psf = ctx.enter_context(tc.psum_pool(name="psf", bufs=1))
         ctx.enter_context(tc.manual_schedule())
 
         wb_t = {}
@@ -132,19 +131,23 @@ def tile_xlstmcell_kernel(tc, x, h_prev, c_prev, W_all_bytes, W_all_scale, b_all
         def quantize(n):
             codes = cpool.tile([P, 1024], U32, name="codes", align_bytes=64)
             scl = cpool.tile([P, 1024], U8, name="scl", align_bytes=64)
-            if n == NG - 1:
-                for i in range(2):
-                    cols = slice(512 * i, 512 * (i + 1))
-                    nc.vector.quantize_mx(
-                        out=codes[:, cols].bitcast(FP8X4),
-                        scales=scl[:, cols],
-                        in_=grp_t[n][:, 2 * i : 2 * i + 2].rearrange("p a g r t -> p (a g r t)"),
-                    )
-            else:
-                nc.vector.quantize_mx(
-                    out=codes[:].bitcast(FP8X4), scales=scl[:], in_=grp_t[n][:].rearrange("p a g r t -> p (a g r t)")
-                )
+            nc.vector.quantize_mx(
+                out=codes[:].bitcast(FP8X4), scales=scl[:], in_=grp_t[n][:].rearrange("p a g r t -> p (a g r t)")
+            )
             cod_t[n] = (codes, scl)
+
+        def quantize_gate(n, i):
+            if i == 0:
+                codes = cpool.tile([P, 1024], U32, name="codes", align_bytes=64)
+                scl = cpool.tile([P, 1024], U8, name="scl", align_bytes=64)
+                cod_t[n] = (codes, scl)
+            codes, scl = cod_t[n]
+            cols = slice(512 * i, 512 * (i + 1))
+            nc.vector.quantize_mx(
+                out=codes[:, cols].bitcast(FP8X4),
+                scales=scl[:, cols],
+                in_=grp_t[n][:, 2 * i : 2 * i + 2].rearrange("p a g r t -> p (a g r t)"),
+            )
 
         def mx_group(out, n, passes):
             codes, scl = cod_t[n]
@@ -166,10 +169,7 @@ def tile_xlstmcell_kernel(tc, x, h_prev, c_prev, W_all_bytes, W_all_scale, b_all
             pr = n % 3
             w_and_u = [(2 + part, 0), (2 + part, 1), (part, 0), (part, 1)]
             if part == 0:
-                if n == NG - 1:
-                    acc = pst.tile([P, 512], F32, name="tp")
-                else:
-                    acc = psa.tile([P, 512], F32, name="acc")
+                acc = psa.tile([P, 512], F32, name="acc")
                 acc_t[n] = [acc]
                 if pr == 0:
                     mx_group(acc[:, 0:B], n, w_and_u[0:2])
@@ -242,10 +242,7 @@ def tile_xlstmcell_kernel(tc, x, h_prev, c_prev, W_all_bytes, W_all_scale, b_all
 
         def finish_tensor(j):
             e = ep_t[j]
-            if j >= NT - 2:
-                tp = pst.tile([P, 512], F32, name="tp")
-            else:
-                tp = psf.tile([P, 512], F32, name="fin")
+            tp = pst.tile([P, 512], F32, name="tp")
             tpv = tp[:].rearrange("p (w t n) -> p w t n", w=2, t=2)
             e["ct"] = tpv[:, 0]
             e["ot"] = tpv[:, 1]
@@ -368,7 +365,7 @@ def tile_xlstmcell_kernel(tc, x, h_prev, c_prev, W_all_bytes, W_all_scale, b_all
                 turn(0, (2, 3))
                 acts.append(prep_quant(xg, "xa"))
                 acts.insert(0, prep_quant(hg, "ha"))
-            if n >= 2 and (n - 4) % 3 != 0 and extra < EARLY:
+            if n >= 2 and (n - 4) % 3 == 2 and extra < EARLY:
                 extra += 1
             while u_done < min(2 * (n + 2) + extra, len(u_units)):
                 turn(u_units[u_done][0], u_units[u_done][1:2])
@@ -408,11 +405,13 @@ def tile_xlstmcell_kernel(tc, x, h_prev, c_prev, W_all_bytes, W_all_scale, b_all
         quantize(NG - 2)
         matmuls(NG - 3, 0)
         matmuls(NG - 3, 1)
-        quantize(NG - 1)
+        quantize_gate(NG - 1, 0)
         gates_scalar(NG - 3)
+        gates_vector(NG - 3)
+        quantize_gate(NG - 1, 1)
         matmuls(NG - 2, 0)
         matmuls(NG - 2, 1)
-        gates_vector(NG - 3)
+        finish_vector(NT - 3)
         gates_vector(NG - 4)
         gates_scalar(NG - 2)
         matmuls(NG - 1, 0)
@@ -421,7 +420,6 @@ def tile_xlstmcell_kernel(tc, x, h_prev, c_prev, W_all_bytes, W_all_scale, b_all
         gates_scalar(NG - 1)
         gates_vector(NG - 1)
         finish_tensor(NT - 2)
-        finish_vector(NT - 3)
         finish_scalar(NT - 2)
         finish_tensor(NT - 1)
         finish_vector(NT - 2)

@@ -88,8 +88,8 @@ def tile_xlstmcell_kernel(tc, x, h_prev, c_prev, W_all_bytes, W_all_scale, b_all
         def product(n):
             wfull = fpool.tile([P, 2, K], BF16, name="wfull")
             if n == 0:
-                for hb in range(2):
-                    cols = slice(512 * hb, 512 * (hb + 1))
+                for a in range(4):
+                    cols = slice(256 * a, 256 * (a + 1))
                     for i in range(2):
                         nc.vector.tensor_tensor(
                             out=wfull[:, i, cols], in0=wb_t[n][:, i, cols].bitcast(FP8), in1=sc2[:, 0, cols], op=ALU.mult
@@ -291,22 +291,25 @@ def tile_xlstmcell_kernel(tc, x, h_prev, c_prev, W_all_bytes, W_all_scale, b_all
         nc.gpsimd.memset(brow[:], 0.0)
 
         sc2 = const.tile([P, 2, K], F32, name="sc2")
-        scol = const.tile([P, 2, 4], F32, name="scol")
-        nc.sync.dma_start(out=scol[:], in_=W_all_scale.rearrange("a b (h p c) -> p (a b h) c", p=P, c=4))
+        scol = const.tile([P, 4, 2], F32, name="scol")
+        nc.sync.dma_start(out=scol[:], in_=W_all_scale.rearrange("x y (a p c) -> p (x y a) c", p=P, c=2))
         load_w(0)
-        load_u(0)
+        load_w(1)
         xraw = const.tile([P, 2, K], BF16, name="xraw")
         nc.sync.dma_start(out=xraw[:], in_=x.rearrange("(t p) k -> p t k", p=P))
         hraw = const.tile([P, 2, K], BF16, name="hraw")
         nc.sync.dma_start(out=hraw[:], in_=h_prev.rearrange("(t p) k -> p t k", p=P))
-        load_w(1)
+        load_u(0)
+        load_w(2)
         load_u(1)
+        nc.sync.dma_start(out=brow[0 : 6 * NT, :], in_=b_all.rearrange("q (j p) -> (q j) p", p=P))
+        load_w(3)
+        load_u(2)
+        load_w(4)
+        load_u(3)
+        load_w(5)
         craw = const.tile([P, 2, H], BF16, name="craw")
         nc.sync.dma_start(out=craw[:], in_=c_prev.rearrange("(t p) n -> p t n", p=P))
-        nc.sync.dma_start(out=brow[0 : 6 * NT, :], in_=b_all.rearrange("q (j p) -> (q j) p", p=P))
-        for n in range(2, AHEAD - 3):
-            load_w(n)
-            load_u(n)
 
         xg = const.tile([P, 2, B, 4], BF16, name="xg", align_bytes=64)
         hg = const.tile([P, 2, B, 4], BF16, name="hg", align_bytes=64)
@@ -333,24 +336,24 @@ def tile_xlstmcell_kernel(tc, x, h_prev, c_prev, W_all_bytes, W_all_scale, b_all
 
         acts = []
 
-        for hb in range(2):
+        for a in range(4):
             tp = pst.tile([P, 512], F32, name="tp")
-            tpv = tp[:].rearrange("p (c n) -> p c n", c=4)
-            for c in range(4):
-                nc.tensor.transpose(tpv[:, c, :], scol[:, hb, c : c + 1].to_broadcast([P, P]), ident[:])
-            dst = sc2[:, 0, 512 * hb : 512 * (hb + 1)].rearrange("p (n c) -> p n c", c=4)
-            if hb == 0:
-                nc.vector.tensor_copy(out=dst, in_=tp[:].rearrange("p (c n) -> p n c", c=4))
+            for c in range(2):
+                nc.tensor.transpose(tp[:, P * c : P * (c + 1)], scol[:, a, c : c + 1].to_broadcast([P, P]), ident[:])
+            dst = sc2[:, 0, 256 * a : 256 * (a + 1)].rearrange("p (n c) -> p n c", c=2)
+            if a == 0:
+                nc.vector.tensor_copy(out=dst, in_=tp[:, 0 : 2 * P].rearrange("p (c n) -> p n c", c=2))
             else:
-                nc.scalar.copy(out=dst, in_=tp[:].rearrange("p (c n) -> p n c", c=4))
+                nc.scalar.copy(out=dst, in_=tp[:, 0 : 2 * P].rearrange("p (c n) -> p n c", c=2))
 
         u_units = [(m, i) for m in range(1, NG) for i in range(2)]
         u_done = 0
         extra = 0
         for n in range(-3, NG - 4):
-            if AHEAD - 3 <= n + AHEAD < NG:
-                load_w(n + AHEAD)
+            if n + AHEAD < NG:
                 load_u(n + AHEAD)
+            if n + AHEAD + 2 < NG:
+                load_w(n + AHEAD + 2)
             if n >= 5 and (n - 5) % 3 == 0:
                 finish_scalar((n - 5) // 3)
             if 0 <= n - 1 < NG:
@@ -358,9 +361,9 @@ def tile_xlstmcell_kernel(tc, x, h_prev, c_prev, W_all_bytes, W_all_scale, b_all
             if 0 <= n + 3 < NG:
                 product(n + 3)
             if n == -3:
-                turn(0, (0, 1))
                 prep_turn(xraw, xg)
                 prep_turn(hraw, hg)
+                turn(0, (0, 1))
             if n == -2:
                 turn(0, (2, 3))
                 acts.append(prep_quant(xg, "xa"))

@@ -24,6 +24,8 @@ GATES = ((4, 5), (0, 3), (1, 2))
 AHEAD = 7
 EARLY = 4
 POS = (0, 2, 1, 3)
+SLOW = (16,)
+TERMS = 3
 
 
 def tile_xlstmcell_kernel(tc, x, h_prev, c_prev, W_all_bytes, W_all_scale, b_all, U_all, out_0, out_1):
@@ -37,7 +39,9 @@ def tile_xlstmcell_kernel(tc, x, h_prev, c_prev, W_all_bytes, W_all_scale, b_all
         cpool = ctx.enter_context(tc.tile_pool(name="cpool", bufs=6))
         epool = ctx.enter_context(tc.tile_pool(name="epool", bufs=2))
         opool = ctx.enter_context(tc.tile_pool(name="opool", bufs=3))
-        pst = ctx.enter_context(tc.psum_pool(name="pst", bufs=5))
+        xpool = ctx.enter_context(tc.tile_pool(name="xpool", bufs=1))
+        pst = ctx.enter_context(tc.psum_pool(name="pst", bufs=4))
+        pfin = ctx.enter_context(tc.psum_pool(name="pfin", bufs=1))
         psa = ctx.enter_context(tc.psum_pool(name="psa", bufs=3))
         ctx.enter_context(tc.manual_schedule())
 
@@ -49,6 +53,8 @@ def tile_xlstmcell_kernel(tc, x, h_prev, c_prev, W_all_bytes, W_all_scale, b_all
         cod_t = {}
         acc_t = {}
         ep_t = {}
+        wex_t = {}
+        vst_t = {}
 
         def gate_rows(dram, n):
             j, pr = divmod(n, 3)
@@ -87,7 +93,12 @@ def tile_xlstmcell_kernel(tc, x, h_prev, c_prev, W_all_bytes, W_all_scale, b_all
 
         def product(n):
             wfull = fpool.tile([P, 2, K], BF16, name="wfull")
-            if n == 0:
+            if n in SLOW:
+                for i in range(2):
+                    nc.vector.tensor_tensor(
+                        out=wfull[:, i, 0:512], in0=wb_t[n][:, i, 0:512].bitcast(FP8), in1=sc2[:, 0, 0:512], op=ALU.mult
+                    )
+            elif n == 0:
                 for a in range(4):
                     cols = slice(256 * a, 256 * (a + 1))
                     for i in range(2):
@@ -108,15 +119,66 @@ def tile_xlstmcell_kernel(tc, x, h_prev, c_prev, W_all_bytes, W_all_scale, b_all
                 )
             wf_t[n] = wfull
 
-        def turn(n, units):
-            if n not in grp_t:
+        def group_tile(n):
+            for m in range(len(grp_t), n + 1):
                 grp = gpool.tile([P, 4, 2, P, 4], BF16, name="grp", align_bytes=64)
-                grp_t[n] = grp
-            grp = grp_t[n]
+                grp_t[m] = grp
+            return grp_t[n]
+
+        def turn_first_half(n):
+            grp = group_tile(n)
+            tp = pst.tile([P, 512], F32, name="tp")
+            for a in range(2):
+                words = wf_t[n][:, a, :].bitcast(F32)
+                for u in range(2):
+                    nc.tensor.transpose(tp[:, P * (2 * a + u) : P * (2 * a + u + 1)], words[:, u:256:2], ident[:])
+            nc.scalar.copy(
+                out=grp[:, 1:4:2, 0].bitcast(F32), in_=tp[:].rearrange("p (a u r) -> p a r u", a=2, u=2)
+            )
+
+        def slow_widen(n):
+            wex = xpool.tile([P, 2, 512], BF16, name="wex")
+            for i in range(2):
+                nc.scalar.copy(out=wex[:, i, :], in_=wb_t[n][:, i, 512:1024].bitcast(FP8))
+            wex_t[n] = wex
+
+        def slow_turn(n):
+            tp = pst.tile([P, 512], F32, name="tp")
+            for u in range(2):
+                for i in range(2):
+                    words = wex_t[n][:, i, :].bitcast(F32)
+                    nc.tensor.transpose(tp[:, P * (2 * u + i) : P * (2 * u + i + 1)], words[:, u:256:2], ident[:])
+            vst = xpool.tile([P, 512], F32, name="vst")
+            nc.scalar.copy(out=vst[:], in_=tp[:])
+            vst_t[n] = vst
+
+        def slow_scale(n, i):
+            grp = group_tile(n)
+            vals = vst_t[n][:].bitcast(BF16)
+            dq = pst.tile([P, 512], F32, name="tp")
+            for t in range(4):
+                u, e = divmod(t, 2)
+                first = 2 * P * (2 * u + i) + e
+                for k in range(TERMS):
+                    nc.tensor.matmul(
+                        out=dq[:, P * t : P * (t + 1)],
+                        lhsT=diag[:, t, k, :],
+                        rhs=vals[:, first : first + 2 * P - 1 : 2],
+                        start=(k == 0),
+                        stop=(k == TERMS - 1),
+                    )
+            nc.scalar.copy(out=grp[:, POS[2 + i], 1], in_=dq[:].rearrange("p (t r) -> p r t", t=4))
+
+        def turn(n, units):
+            grp = group_tile(n)
             for unit in units:
                 if (n, unit) in turned:
                     continue
                 turned.add((n, unit))
+                if n in SLOW and unit >= 2:
+                    if unit == 2:
+                        turn_first_half(n)
+                    continue
                 src = ub_t[n] if unit < 2 else wf_t[n]
                 words = src[:, unit % 2, :].bitcast(F32)
                 tp = pst.tile([P, 512], F32, name="tp")
@@ -242,7 +304,10 @@ def tile_xlstmcell_kernel(tc, x, h_prev, c_prev, W_all_bytes, W_all_scale, b_all
 
         def finish_tensor(j):
             e = ep_t[j]
-            tp = pst.tile([P, 512], F32, name="tp")
+            if j < NT - 2:
+                tp = pfin.tile([P, 512], F32, name="fin")
+            else:
+                tp = pst.tile([P, 512], F32, name="tp")
             tpv = tp[:].rearrange("p (w t n) -> p w t n", w=2, t=2)
             e["ct"] = tpv[:, 0]
             e["ot"] = tpv[:, 1]
@@ -311,6 +376,24 @@ def tile_xlstmcell_kernel(tc, x, h_prev, c_prev, W_all_bytes, W_all_scale, b_all
         craw = const.tile([P, 2, H], BF16, name="craw")
         nc.sync.dma_start(out=craw[:], in_=c_prev.rearrange("(t p) n -> p t n", p=P))
 
+        st = const.tile([P, 2, 4], F32, name="st")
+        nc.sync.dma_start(out=st[:], in_=W_all_scale.rearrange("x y (g p t) -> p (x y g) t", p=P, t=4))
+        piece = const.tile([P, TERMS, 4], F32, name="piece")
+        round_t = const.tile([P, TERMS, 4], BF16, name="round_t")
+        diag = const.tile([P, 4, TERMS, P], BF16, name="diag")
+
+        def split_scales(k):
+            if k == 0:
+                nc.scalar.copy(out=piece[:, 0, :], in_=st[:, 1, :])
+            else:
+                nc.scalar.copy(out=round_t[:, k - 1, :], in_=piece[:, k - 1, :])
+                nc.gpsimd.tensor_tensor(
+                    out=piece[:, k, :], in0=piece[:, k - 1, :], in1=round_t[:, k - 1, :], op=ALU.subtract
+                )
+
+        def make_diag(t, k):
+            nc.scalar.activation(out=diag[:, t, k, :], in_=identb[:], func=ACT.Copy, scale=piece[:, k, t : t + 1])
+
         xg = const.tile([P, 2, B, 4], BF16, name="xg", align_bytes=64)
         hg = const.tile([P, 2, B, 4], BF16, name="hg", align_bytes=64)
         y3 = const.tile([P, NT, 3, B], F32, name="y3")
@@ -373,10 +456,23 @@ def tile_xlstmcell_kernel(tc, x, h_prev, c_prev, W_all_bytes, W_all_scale, b_all
             while u_done < min(2 * (n + 2) + extra, len(u_units)):
                 turn(u_units[u_done][0], u_units[u_done][1:2])
                 u_done += 1
+            if n + 6 in SLOW:
+                slow_turn(n + 6)
             if 0 <= n < NG:
                 matmuls(n, 0)
+            if n + 5 in SLOW:
+                slow_scale(n + 5, 0)
+            if n + 4 in SLOW:
+                slow_scale(n + 4, 1)
             if 1 <= n + 2 < NG:
                 turn(n + 2, (2, 3))
+            if n + 7 in SLOW:
+                slow_widen(n + 7)
+            if 3 <= n < 3 + TERMS:
+                split_scales(n - 3)
+            if 4 <= n < 4 + 2 * TERMS:
+                for t in range(2 * (n % 2), 2 * (n % 2) + 2):
+                    make_diag(t, (n - 4) // 2)
             if n == -1:
                 turn_b()
             if n == 1:

@@ -24,8 +24,7 @@ GATES = ((4, 5), (0, 3), (1, 2))
 AHEAD = 7
 EARLY = 4
 POS = (0, 2, 1, 3)
-SLOW = (16,)
-TERMS = 3
+SLOW = (11, 19)
 
 
 def tile_xlstmcell_kernel(tc, x, h_prev, c_prev, W_all_bytes, W_all_scale, b_all, U_all, out_0, out_1):
@@ -152,22 +151,17 @@ def tile_xlstmcell_kernel(tc, x, h_prev, c_prev, W_all_bytes, W_all_scale, b_all
             nc.scalar.copy(out=vst[:], in_=tp[:])
             vst_t[n] = vst
 
-        def slow_scale(n, i):
+        def slow_scale(n, t):
             grp = group_tile(n)
             vals = vst_t[n][:].bitcast(BF16)
-            dq = pst.tile([P, 512], F32, name="tp")
-            for t in range(4):
-                u, e = divmod(t, 2)
-                first = 2 * P * (2 * u + i) + e
-                for k in range(TERMS):
-                    nc.tensor.matmul(
-                        out=dq[:, P * t : P * (t + 1)],
-                        lhsT=diag[:, t, k, :],
-                        rhs=vals[:, first : first + 2 * P - 1 : 2],
-                        start=(k == 0),
-                        stop=(k == TERMS - 1),
-                    )
-            nc.scalar.copy(out=grp[:, POS[2 + i], 1], in_=dq[:].rearrange("p (t r) -> p r t", t=4))
+            u, e = divmod(t, 2)
+            first = 4 * P * u + e
+            nc.scalar.activation(
+                out=grp[:, 1:4:2, 1, :, t],
+                in_=vals[:, first : first + 4 * P - 1 : 2].rearrange("p (i r) -> p i r", i=2),
+                func=ACT.Copy,
+                scale=st[:, 1, t : t + 1],
+            )
 
         def turn(n, units):
             grp = group_tile(n)
@@ -378,22 +372,6 @@ def tile_xlstmcell_kernel(tc, x, h_prev, c_prev, W_all_bytes, W_all_scale, b_all
 
         st = const.tile([P, 2, 4], F32, name="st")
         nc.sync.dma_start(out=st[:], in_=W_all_scale.rearrange("x y (g p t) -> p (x y g) t", p=P, t=4))
-        piece = const.tile([P, TERMS, 4], F32, name="piece")
-        round_t = const.tile([P, TERMS, 4], BF16, name="round_t")
-        diag = const.tile([P, 4, TERMS, P], BF16, name="diag")
-
-        def split_scales(k):
-            if k == 0:
-                nc.scalar.copy(out=piece[:, 0, :], in_=st[:, 1, :])
-            else:
-                nc.scalar.copy(out=round_t[:, k - 1, :], in_=piece[:, k - 1, :])
-                nc.gpsimd.tensor_tensor(
-                    out=piece[:, k, :], in0=piece[:, k - 1, :], in1=round_t[:, k - 1, :], op=ALU.subtract
-                )
-
-        def make_diag(t, k):
-            nc.scalar.activation(out=diag[:, t, k, :], in_=identb[:], func=ACT.Copy, scale=piece[:, k, t : t + 1])
-
         xg = const.tile([P, 2, B, 4], BF16, name="xg", align_bytes=64)
         hg = const.tile([P, 2, B, 4], BF16, name="hg", align_bytes=64)
         y3 = const.tile([P, NT, 3, B], F32, name="y3")
@@ -460,19 +438,13 @@ def tile_xlstmcell_kernel(tc, x, h_prev, c_prev, W_all_bytes, W_all_scale, b_all
                 slow_turn(n + 6)
             if 0 <= n < NG:
                 matmuls(n, 0)
-            if n + 5 in SLOW:
-                slow_scale(n + 5, 0)
-            if n + 4 in SLOW:
-                slow_scale(n + 4, 1)
             if 1 <= n + 2 < NG:
                 turn(n + 2, (2, 3))
             if n + 7 in SLOW:
                 slow_widen(n + 7)
-            if 3 <= n < 3 + TERMS:
-                split_scales(n - 3)
-            if 4 <= n < 4 + 2 * TERMS:
-                for t in range(2 * (n % 2), 2 * (n % 2) + 2):
-                    make_diag(t, (n - 4) // 2)
+            for t in range(4):
+                if n + 5 - t in SLOW:
+                    slow_scale(n + 5 - t, t)
             if n == -1:
                 turn_b()
             if n == 1:

@@ -24,7 +24,7 @@ GATES = ((4, 5), (0, 3), (1, 2))
 AHEAD = 7
 EARLY = 4
 POS = (0, 2, 1, 3)
-SLOW = (11, 19)
+SLOW = (8, 12, 16, 20)
 
 
 def tile_xlstmcell_kernel(tc, x, h_prev, c_prev, W_all_bytes, W_all_scale, b_all, U_all, out_0, out_1):
@@ -135,11 +135,11 @@ def tile_xlstmcell_kernel(tc, x, h_prev, c_prev, W_all_bytes, W_all_scale, b_all
                 out=grp[:, 1:4:2, 0].bitcast(F32), in_=tp[:].rearrange("p (a u r) -> p a r u", a=2, u=2)
             )
 
-        def slow_widen(n):
-            wex = xpool.tile([P, 2, 512], BF16, name="wex")
-            for i in range(2):
-                nc.scalar.copy(out=wex[:, i, :], in_=wb_t[n][:, i, 512:1024].bitcast(FP8))
-            wex_t[n] = wex
+        def slow_widen(n, i):
+            if i == 0:
+                wex = xpool.tile([P, 2, 512], BF16, name="wex")
+                wex_t[n] = wex
+            nc.scalar.copy(out=wex_t[n][:, i, :], in_=wb_t[n][:, i, 512:1024].bitcast(FP8))
 
         def slow_turn(n):
             tp = pst.tile([P, 512], F32, name="tp")
@@ -147,21 +147,19 @@ def tile_xlstmcell_kernel(tc, x, h_prev, c_prev, W_all_bytes, W_all_scale, b_all
                 for i in range(2):
                     words = wex_t[n][:, i, :].bitcast(F32)
                     nc.tensor.transpose(tp[:, P * (2 * u + i) : P * (2 * u + i + 1)], words[:, u:256:2], ident[:])
-            vst = xpool.tile([P, 512], F32, name="vst")
-            nc.scalar.copy(out=vst[:], in_=tp[:])
-            vst_t[n] = vst
+            planes = xpool.tile([P, 4, 2 * P], BF16, name="planes")
+            vals = tp[:].bitcast(BF16)
+            for t in range(4):
+                u, e = divmod(t, 2)
+                first = 4 * P * u + e
+                nc.scalar.activation(
+                    out=planes[:, t, :], in_=vals[:, first : first + 4 * P - 1 : 2], func=ACT.Copy, scale=st[:, 1, t : t + 1]
+                )
+            vst_t[n] = planes
 
-        def slow_scale(n, t):
+        def slow_weave(n):
             grp = group_tile(n)
-            vals = vst_t[n][:].bitcast(BF16)
-            u, e = divmod(t, 2)
-            first = 4 * P * u + e
-            nc.scalar.activation(
-                out=grp[:, 1:4:2, 1, :, t],
-                in_=vals[:, first : first + 4 * P - 1 : 2].rearrange("p (i r) -> p i r", i=2),
-                func=ACT.Copy,
-                scale=st[:, 1, t : t + 1],
-            )
+            nc.scalar.copy(out=grp[:, 1:4:2, 1], in_=vst_t[n][:].rearrange("p t (i r) -> p i r t", i=2))
 
         def turn(n, units):
             grp = group_tile(n)
@@ -434,17 +432,18 @@ def tile_xlstmcell_kernel(tc, x, h_prev, c_prev, W_all_bytes, W_all_scale, b_all
             while u_done < min(2 * (n + 2) + extra, len(u_units)):
                 turn(u_units[u_done][0], u_units[u_done][1:2])
                 u_done += 1
-            if n + 6 in SLOW:
-                slow_turn(n + 6)
+            if n + 4 in SLOW:
+                slow_turn(n + 4)
             if 0 <= n < NG:
                 matmuls(n, 0)
             if 1 <= n + 2 < NG:
                 turn(n + 2, (2, 3))
-            if n + 7 in SLOW:
-                slow_widen(n + 7)
-            for t in range(4):
-                if n + 5 - t in SLOW:
-                    slow_scale(n + 5 - t, t)
+            if n + 6 in SLOW:
+                slow_widen(n + 6, 0)
+            if n + 5 in SLOW:
+                slow_widen(n + 5, 1)
+            if n + 3 in SLOW:
+                slow_weave(n + 3)
             if n == -1:
                 turn_b()
             if n == 1:

@@ -39,6 +39,7 @@ def tile_xlstmcell_kernel(tc, x, h_prev, c_prev, W_all_bytes, W_all_scale, b_all
         epool = ctx.enter_context(tc.tile_pool(name="epool", bufs=2))
         opool = ctx.enter_context(tc.tile_pool(name="opool", bufs=3))
         xpool = ctx.enter_context(tc.tile_pool(name="xpool", bufs=1))
+        dpool = ctx.enter_context(tc.tile_pool(name="dpool", bufs=1))
         pst = ctx.enter_context(tc.psum_pool(name="pst", bufs=4))
         pfin = ctx.enter_context(tc.psum_pool(name="pfin", bufs=1))
         psa = ctx.enter_context(tc.psum_pool(name="psa", bufs=3))
@@ -413,6 +414,9 @@ def tile_xlstmcell_kernel(tc, x, h_prev, c_prev, W_all_bytes, W_all_scale, b_all
                 load_u(n + AHEAD)
             if n + AHEAD + 2 < NG:
                 load_w(n + AHEAD + 2)
+            if 2 <= n <= 16 and n % 2 == 0:
+                again = dpool.tile([P, 2, K], BF16, name="again")
+                nc.sync.dma_start(out=again[:], in_=gate_rows(U_all, n))
             if n >= 5 and (n - 5) % 3 == 0:
                 finish_scalar((n - 5) // 3)
             if 0 <= n - 1 < NG:

from contextlib import ExitStack

import concourse.mybir as mybir
from concourse.masks import make_identity

FLOPS = 2 * 256 * 1024 * 1024 * 12

F32 = mybir.dt.float32
BF16 = mybir.dt.bfloat16
U32 = mybir.dt.uint32
U8 = mybir.dt.uint8
FP8 = mybir.dt.float8_e4m3fn
FP8X4 = mybir.dt.float8_e4m3fn_x4
ACT = mybir.ActivationFunctionType
ALU = mybir.AluOpType

P = 128
B = 256
K = 1024
H = 1024
NT = H // P
NG = 3 * NT
GATES = ((4, 5), (0, 3), (1, 2))
AHEAD = 7
EARLY = 4
POS = (0, 2, 1, 3)
SLOW = (8, 12, 16, 20)


def tile_xlstmcell_kernel(tc, x, h_prev, c_prev, W_all_bytes, W_all_scale, b_all, U_all, out_0, out_1):
    nc = tc.nc
    with ExitStack() as ctx:
        const = ctx.enter_context(tc.tile_pool(name="const", bufs=1))
        wpool = ctx.enter_context(tc.tile_pool(name="wpool", bufs=8))
        upool = ctx.enter_context(tc.tile_pool(name="upool", bufs=8))
        fpool = ctx.enter_context(tc.tile_pool(name="fpool", bufs=4))
        gpool = ctx.enter_context(tc.tile_pool(name="gpool", bufs=6))
        cpool = ctx.enter_context(tc.tile_pool(name="cpool", bufs=6))
        epool = ctx.enter_context(tc.tile_pool(name="epool", bufs=2))
        opool = ctx.enter_context(tc.tile_pool(name="opool", bufs=3))
        xpool = ctx.enter_context(tc.tile_pool(name="xpool", bufs=1))
        dpool = ctx.enter_context(tc.tile_pool(name="dpool", bufs=1))
        pst = ctx.enter_context(tc.psum_pool(name="pst", bufs=4))
        pfin = ctx.enter_context(tc.psum_pool(name="pfin", bufs=1))
        psa = ctx.enter_context(tc.psum_pool(name="psa", bufs=3))
        ctx.enter_context(tc.manual_schedule())

        wb_t = {}
        ub_t = {}
        wf_t = {}
        grp_t = {}
        turned = set()
        cod_t = {}
        acc_t = {}
        ep_t = {}
        wex_t = {}
        vst_t = {}

        def gate_rows(dram, n):
            j, pr = divmod(n, 3)
            a, b = GATES[pr]
            return dram[a : b + 1 : b - a, P * j : P * (j + 1), :].rearrange("q p k -> p q k")

        def load_w(n):
            wbytes = wpool.tile([P, 2, K], U8, name="wbytes")
            nc.sync.dma_start(out=wbytes[:], in_=gate_rows(W_all_bytes, n))
            wb_t[n] = wbytes

        def load_u(n):
            ubf = upool.tile([P, 2, K], BF16, name="ubf")
            nc.sync.dma_start(out=ubf[:], in_=gate_rows(U_all, n))
            ub_t[n] = ubf

        def prep_turn(raw, ag):
            for g in range(2):
                tp = pst.tile([P, 512], F32, name="tp")
                tpv = tp[:].rearrange("p (u b) -> p u b", u=2)
                for bt in range(2):
                    words = raw[:, bt, :].bitcast(F32)
                    for u in range(2):
                        nc.tensor.transpose(
                            tpv[:, u, P * bt : P * (bt + 1)], words[:, 256 * g + u : 256 * (g + 1) : 2], ident[:]
                        )
                nc.scalar.copy(out=ag[:, g].bitcast(F32), in_=tp[:].rearrange("p (u b) -> p b u", u=2))

        def prep_quant(ag, nm):
            ac = const.tile([P, 2 * B], U32, name=nm + "c", align_bytes=64)
            asc = const.tile([P, 2 * B], U8, name=nm + "s", align_bytes=64)
            nc.vector.quantize_mx(
                out=ac[:].bitcast(FP8X4), scales=asc[:], in_=ag[:].rearrange("p g b t -> p (g b t)")
            )
            return ac, asc

        def product(n):
            wfull = fpool.tile([P, 2, K], BF16, name="wfull")
            if n in SLOW:
                for i in range(2):
                    nc.vector.tensor_tensor(
                        out=wfull[:, i, 0:512], in0=wb_t[n][:, i, 0:512].bitcast(FP8), in1=sc2[:, 0, 0:512], op=ALU.mult
                    )
            elif n == 0:
                for a in range(4):
                    cols = slice(256 * a, 256 * (a + 1))
                    for i in range(2):
                        nc.vector.tensor_tensor(
                            out=wfull[:, i, cols], in0=wb_t[n][:, i, cols].bitcast(FP8), in1=sc2[:, 0, cols], op=ALU.mult
                        )
            elif n < 5 or n == NG - 1:
                for i in range(2):
                    nc.vector.tensor_tensor(
                        out=wfull[:, i, :], in0=wb_t[n][:, i, :].bitcast(FP8), in1=sc2[:, 0, :], op=ALU.mult
                    )
            else:
                nc.vector.tensor_tensor(
                    out=wfull[:].rearrange("p q k -> p (q k)"),
                    in0=wb_t[n][:].rearrange("p q k -> p (q k)").bitcast(FP8),
                    in1=sc2[:].rearrange("p a k -> p (a k)"),
                    op=ALU.mult,
                )
            wf_t[n] = wfull

        def group_tile(n):
            for m in range(len(grp_t), n + 1):
                grp = gpool.tile([P, 4, 2, P, 4], BF16, name="grp", align_bytes=64)
                grp_t[m] = grp
            return grp_t[n]

        def turn_first_half(n):
            grp = group_tile(n)
            tp = pst.tile([P, 512], F32, name="tp")
            for a in range(2):
                words = wf_t[n][:, a, :].bitcast(F32)
                for u in range(2):
                    nc.tensor.transpose(tp[:, P * (2 * a + u) : P * (2 * a + u + 1)], words[:, u:256:2], ident[:])
            nc.scalar.copy(
                out=grp[:, 1:4:2, 0].bitcast(F32), in_=tp[:].rearrange("p (a u r) -> p a r u", a=2, u=2)
            )

        def slow_widen(n, i):
            if i == 0:
                wex = xpool.tile([P, 2, 512], BF16, name="wex")
                wex_t[n] = wex
            nc.scalar.copy(out=wex_t[n][:, i, :], in_=wb_t[n][:, i, 512:1024].bitcast(FP8))

        def slow_turn(n):
            tp = pst.tile([P, 512], F32, name="tp")
            for u in range(2):
                for i in range(2):
                    words = wex_t[n][:, i, :].bitcast(F32)
                    nc.tensor.transpose(tp[:, P * (2 * u + i) : P * (2 * u + i + 1)], words[:, u:256:2], ident[:])
            planes = xpool.tile([P, 4, 2 * P], BF16, name="planes")
            vals = tp[:].bitcast(BF16)
            for t in range(4):
                u, e = divmod(t, 2)
                first = 4 * P * u + e
                nc.scalar.activation(
                    out=planes[:, t, :], in_=vals[:, first : first + 4 * P - 1 : 2], func=ACT.Copy, scale=st[:, 1, t : t + 1]
                )
            vst_t[n] = planes

        def slow_weave(n):
            grp = group_tile(n)
            nc.scalar.copy(out=grp[:, 1:4:2, 1], in_=vst_t[n][:].rearrange("p t (i r) -> p i r t", i=2))

        def turn(n, units):
            grp = group_tile(n)
            for unit in units:
                if (n, unit) in turned:
                    continue
                turned.add((n, unit))
                if n in SLOW and unit >= 2:
                    if unit == 2:
                        turn_first_half(n)
                    continue
                src = ub_t[n] if unit < 2 else wf_t[n]
                words = src[:, unit % 2, :].bitcast(F32)
                tp = pst.tile([P, 512], F32, name="tp")
                tpv = tp[:].rearrange("p (g u r) -> p g u r", g=2, u=2)
                for g in range(2):
                    for u in range(2):
                        nc.tensor.transpose(tpv[:, g, u, :], words[:, 256 * g + u : 256 * (g + 1) : 2], ident[:])
                nc.scalar.copy(
                    out=grp[:, POS[unit]].bitcast(F32), in_=tp[:].rearrange("p (g u r) -> p g r u", g=2, u=2)
                )

        def quantize(n):
            codes = cpool.tile([P, 1024], U32, name="codes", align_bytes=64)
            scl = cpool.tile([P, 1024], U8, name="scl", align_bytes=64)
            nc.vector.quantize_mx(
                out=codes[:].bitcast(FP8X4), scales=scl[:], in_=grp_t[n][:].rearrange("p a g r t -> p (a g r t)")
            )
            cod_t[n] = (codes, scl)

        def quantize_gate(n, i):
            if i == 0:
                codes = cpool.tile([P, 1024], U32, name="codes", align_bytes=64)
                scl = cpool.tile([P, 1024], U8, name="scl", align_bytes=64)
                cod_t[n] = (codes, scl)
            codes, scl = cod_t[n]
            cols = slice(512 * i, 512 * (i + 1))
            nc.vector.quantize_mx(
                out=codes[:, cols].bitcast(FP8X4),
                scales=scl[:, cols],
                in_=grp_t[n][:, 2 * i : 2 * i + 2].rearrange("p a g r t -> p (a g r t)"),
            )

        def mx_group(out, n, passes):
            codes, scl = cod_t[n]
            last = len(passes) - 1
            for idx, (unit, g) in enumerate(passes):
                ac, asc = acts[unit // 2]
                off = (POS[unit] * 2 + g) * P
                nc.tensor.matmul_mx(
                    out=out,
                    lhsT=codes[:, off : off + P].bitcast(FP8X4),
                    lhsT_scale=scl[:, off : off + P],
                    rhs=ac[:, g * B : (g + 1) * B].bitcast(FP8X4),
                    rhs_scale=asc[:, g * B : (g + 1) * B],
                    start=(idx == 0),
                    stop=(idx == last),
                )

        def matmuls(n, part):
            pr = n % 3
            w_and_u = [(2 + part, 0), (2 + part, 1), (part, 0), (part, 1)]
            if part == 0:
                acc = psa.tile([P, 512], F32, name="acc")
                acc_t[n] = [acc]
                if pr == 0:
                    mx_group(acc[:, 0:B], n, w_and_u[0:2])
                    mx_group(acc[:, B : 2 * B], n, w_and_u[2:4])
                else:
                    mx_group(acc[:, 0:B], n, w_and_u)
            elif pr == 0:
                acc2 = psa.tile([P, 512], F32, name="acc")
                acc_t[n].append(acc2)
                mx_group(acc2[:, 0:B], n, w_and_u)
            else:
                mx_group(acc_t[n][0][:, B : 2 * B], n, w_and_u)

        def gate_act(out, src, q, j):
            col = q * NT + j
            func = ACT.Tanh if q == 3 else ACT.Sigmoid
            nc.scalar.activation(out=out, in_=src, func=func, bias=bfull[:, col : col + 1], scale=1.0)

        def gates_scalar(n):
            j, pr = divmod(n, 3)
            e = ep_t.setdefault(j, {})
            acc = acc_t[n][0]
            if pr == 0:
                s3 = epool.tile([P, 3, B], F32, name="s3")
                e["s3"] = s3
                u4 = epool.tile([P, B], F32, name="u4")
                e["u4"] = u4
                nc.scalar.copy(out=u4[:], in_=acc[:, B : 2 * B])
                gate_act(s3[:, 2, :], acc_t[n][1][:, 0:B], 5, j)
            elif pr == 1:
                gate_act(e["s3"][:, 1, :], acc[:, 0:B], 0, j)
                gate_act(y3[:, j, 1, :], acc[:, B : 2 * B], 3, j)
            else:
                gate_act(e["s3"][:, 0, :], acc[:, 0:B], 1, j)
                so = epool.tile([P, B], F32, name="so")
                e["so"] = so
                gate_act(so[:], acc[:, B : 2 * B], 2, j)

        def gate_times(j, lo, hi):
            e = ep_t[j]
            nc.vector.tensor_tensor(
                out=e["p3"][:, lo:hi, :].rearrange("p w b -> p (w b)"),
                in0=e["s3"][:, lo:hi, :].rearrange("p w b -> p (w b)"),
                in1=y3[:, j, lo:hi, :].rearrange("p w b -> p (w b)"),
                op=ALU.mult,
            )

        def gates_vector(n):
            j, pr = divmod(n, 3)
            e = ep_t[j]
            if pr == 0:
                col = 4 * NT + j
                nc.vector.scalar_tensor_tensor(
                    out=y3[:, j, 2, :],
                    in0=acc_t[n][0][:, 0:B],
                    scalar=bfull[:, col : col + 1],
                    in1=e["u4"][:],
                    op0=ALU.add,
                    op1=ALU.mult,
                )
                p3 = epool.tile([P, 3, B], F32, name="p3")
                e["p3"] = p3
            elif j == NT - 1:
                if pr == 1:
                    gate_times(j, 1, 3)
                else:
                    gate_times(j, 0, 1)
            elif pr == 2:
                gate_times(j, 0, 3)

        def finish_tensor(j):
            e = ep_t[j]
            if j < NT - 2:
                tp = pfin.tile([P, 512], F32, name="fin")
            else:
                tp = pst.tile([P, 512], F32, name="tp")
            tpv = tp[:].rearrange("p (w t n) -> p w t n", w=2, t=2)
            e["ct"] = tpv[:, 0]
            e["ot"] = tpv[:, 1]
            if j == NT - 1:
                tpo = pst.tile([P, 512], F32, name="tp")
                e["ot"] = tpo[:].rearrange("p (w t n) -> p w t n", w=2, t=2)[:, 0]
            for bt in range(2):
                nc.tensor.transpose(e["ot"][:, bt, :], e["so"][:, P * bt : P * (bt + 1)], ident[:])
            for bt in range(2):
                for idx, w in enumerate((1, 2, 0)):
                    nc.tensor.matmul(
                        out=e["ct"][:, bt, :],
                        lhsT=e["p3"][:, w, P * bt : P * (bt + 1)],
                        rhs=ident[:],
                        is_transpose=True,
                        start=(idx == 0),
                        stop=(idx == 2),
                    )

        def finish_scalar(j):
            e = ep_t[j]
            tcn = epool.tile([P, 2, P], F32, name="tcn")
            nc.scalar.activation(out=tcn[:], in_=e["ct"], func=ACT.Tanh)
            co = opool.tile([P, 2, P], F32, name="co")
            nc.scalar.copy(out=co[:], in_=e["ct"])
            cols = slice(P * j, P * (j + 1))
            nc.sync.dma_start(out=out_1.rearrange("(t p) n -> p t n", p=P)[:, :, cols], in_=co[:])
            e["tcn"] = tcn

        def finish_vector(j):
            e = ep_t[j]
            ho = opool.tile([P, 2, P], F32, name="ho")
            nc.vector.tensor_tensor(out=ho[:], in0=e["ot"], in1=e["tcn"][:], op=ALU.mult)
            cols = slice(P * j, P * (j + 1))
            nc.sync.dma_start(out=out_0.rearrange("(t p) n -> p t n", p=P)[:, :, cols], in_=ho[:])

        warm = const.tile([P, 1], F32, name="warm")
        warm2 = const.tile([P, 1], F32, name="warm2")
        nc.vector.memset(warm[:], 0.0)
        nc.scalar.activation(out=warm2[:], in_=warm[:], func=ACT.Sigmoid)
        ident = const.tile([P, P], F32, name="ident")
        make_identity(nc, ident[:])
        identb = const.tile([P, P], BF16, name="identb")
        make_identity(nc, identb[:])
        brow = const.tile([P, P], BF16, name="brow")
        nc.gpsimd.memset(brow[:], 0.0)

        sc2 = const.tile([P, 2, K], F32, name="sc2")
        scol = const.tile([P, 4, 2], F32, name="scol")
        nc.sync.dma_start(out=scol[:], in_=W_all_scale.rearrange("x y (a p c) -> p (x y a) c", p=P, c=2))
        load_w(0)
        load_w(1)
        xraw = const.tile([P, 2, K], BF16, name="xraw")
        nc.sync.dma_start(out=xraw[:], in_=x.rearrange("(t p) k -> p t k", p=P))
        hraw = const.tile([P, 2, K], BF16, name="hraw")
        nc.sync.dma_start(out=hraw[:], in_=h_prev.rearrange("(t p) k -> p t k", p=P))
        load_u(0)
        load_w(2)
        load_u(1)
        nc.sync.dma_start(out=brow[0 : 6 * NT, :], in_=b_all.rearrange("q (j p) -> (q j) p", p=P))
        load_w(3)
        load_u(2)
        load_w(4)
        load_u(3)
        load_w(5)
        craw = const.tile([P, 2, H], BF16, name="craw")
        nc.sync.dma_start(out=craw[:], in_=c_prev.rearrange("(t p) n -> p t n", p=P))

        st = const.tile([P, 2, 4], F32, name="st")
        nc.sync.dma_start(out=st[:], in_=W_all_scale.rearrange("x y (g p t) -> p (x y g) t", p=P, t=4))
        xg = const.tile([P, 2, B, 4], BF16, name="xg", align_bytes=64)
        hg = const.tile([P, 2, B, 4], BF16, name="hg", align_bytes=64)
        y3 = const.tile([P, NT, 3, B], F32, name="y3")
        bfull = const.tile([P, 6 * NT], F32, name="bfull")

        def turn_c():
            for half in range(2):
                tpb = pst.tile([P, 1024], BF16, name="tp")
                tpbv = tpb[:].rearrange("p (j b) -> p j b", j=4)
                for jj in range(4):
                    for bt in range(2):
                        nc.tensor.transpose(
                            tpbv[:, jj, P * bt : P * (bt + 1)],
                            craw[:, bt, P * (4 * half + jj) : P * (4 * half + jj + 1)],
                            identb[:],
                        )
                nc.scalar.copy(out=y3[:, 4 * half : 4 * half + 4, 0, :], in_=tpbv)

        def turn_b():
            tpb = pst.tile([P, 1024], BF16, name="tp")
            nc.tensor.transpose(tpb[:, 0:P], brow[:], identb[:])
            nc.scalar.copy(out=bfull[:], in_=tpb[:, 0 : 6 * NT])

        acts = []

        for a in range(4):
            tp = pst.tile([P, 512], F32, name="tp")
            for c in range(2):
                nc.tensor.transpose(tp[:, P * c : P * (c + 1)], scol[:, a, c : c + 1].to_broadcast([P, P]), ident[:])
            dst = sc2[:, 0, 256 * a : 256 * (a + 1)].rearrange("p (n c) -> p n c", c=2)
            if a == 0:
                nc.vector.tensor_copy(out=dst, in_=tp[:, 0 : 2 * P].rearrange("p (c n) -> p n c", c=2))
            else:
                nc.scalar.copy(out=dst, in_=tp[:, 0 : 2 * P].rearrange("p (c n) -> p n c", c=2))

        u_units = [(m, i) for m in range(1, NG) for i in range(2)]
        u_done = 0
        extra = 0
        for n in range(-3, NG - 4):
            if n + AHEAD < NG:
                load_u(n + AHEAD)
            if n + AHEAD + 2 < NG:
                load_w(n + AHEAD + 2)
            if 2 <= n <= 16 and n % 2 == 0:
                again = dpool.tile([P, 2, K], BF16, name="again")
                nc.sync.dma_start(out=again[:], in_=gate_rows(U_all, n))
            if n >= 5 and (n - 5) % 3 == 0:
                finish_scalar((n - 5) // 3)
            if 0 <= n - 1 < NG:
                gates_scalar(n - 1)
            if 0 <= n + 3 < NG:
                product(n + 3)
            if n == -3:
                prep_turn(xraw, xg)
                prep_turn(hraw, hg)
                turn(0, (0, 1))
            if n == -2:
                turn(0, (2, 3))
                acts.append(prep_quant(xg, "xa"))
                acts.insert(0, prep_quant(hg, "ha"))
            if n >= 2 and (n - 4) % 3 == 2 and extra < EARLY:
                extra += 1
            while u_done < min(2 * (n + 2) + extra, len(u_units)):
                turn(u_units[u_done][0], u_units[u_done][1:2])
                u_done += 1
            if n + 4 in SLOW:
                slow_turn(n + 4)
            if 0 <= n < NG:
                matmuls(n, 0)
            if 1 <= n + 2 < NG:
                turn(n + 2, (2, 3))
            if n + 6 in SLOW:
                slow_widen(n + 6, 0)
            if n + 5 in SLOW:
                slow_widen(n + 5, 1)
            if n + 3 in SLOW:
                slow_weave(n + 3)
            if n == -1:
                turn_b()
            if n == 1:
                nc.scalar.copy(out=sc2[:, 1, :], in_=sc2[:, 0, :])
            if n == 2:
                turn_c()
            if n >= 4 and (n - 4) % 3 == 0 and (n - 4) // 3 < NT:
                finish_tensor((n - 4) // 3)
            if 0 <= n + 1 < NG:
                quantize(n + 1)
            if 0 <= n < NG:
                matmuls(n, 1)
            if 0 <= n - 1 < NG:
                gates_vector(n - 1)
            if n >= 5 and (n - 5) % 3 == 0:
                finish_vector((n - 5) // 3)

        finish_scalar(NT - 3)
        gates_scalar(NG - 5)
        product(NG - 1)
        turn(NG - 2, (0, 1))
        matmuls(NG - 4, 0)
        turn(NG - 2, (2, 3))
        quantize(NG - 3)
        matmuls(NG - 4, 1)
        gates_scalar(NG - 4)
        turn(NG - 1, (0, 2))
        turn(NG - 1, (1, 3))
        quantize(NG - 2)
        matmuls(NG - 3, 0)
        matmuls(NG - 3, 1)
        quantize_gate(NG - 1, 0)
        gates_scalar(NG - 3)
        gates_vector(NG - 3)
        quantize_gate(NG - 1, 1)
        matmuls(NG - 2, 0)
        matmuls(NG - 2, 1)
        finish_vector(NT - 3)
        gates_vector(NG - 4)
        gates_scalar(NG - 2)
        matmuls(NG - 1, 0)
        matmuls(NG - 1, 1)
        gates_vector(NG - 2)
        gates_scalar(NG - 1)
        gates_vector(NG - 1)
        finish_tensor(NT - 2)
        finish_scalar(NT - 2)
        finish_tensor(NT - 1)
        finish_vector(NT - 2)
        finish_scalar(NT - 1)
        finish_vector(NT - 1)
